import numpy as np
import ml_dtypes


def mxq(x, axis, fmt="e4m3"):
    dtype, down = {"e4m3": (ml_dtypes.float8_e4m3fn, 7), "e5m2": (ml_dtypes.float8_e5m2, 14)}[fmt]
    v = np.moveaxis(np.asarray(x, np.float32).astype(ml_dtypes.bfloat16).astype(np.float64), axis, -1)
    blocks = v.reshape(v.shape[:-1] + (-1, 32))
    amax = np.abs(blocks).max(-1, keepdims=True)
    byte = np.maximum(np.where(amax > 0, np.frexp(amax)[1] - 1 + 127, 0) - down, 1)
    scale = np.exp2(byte - 127.0)
    codes = (blocks / scale).astype(np.float32).astype(dtype).astype(np.float64)
    return np.moveaxis((codes * scale).reshape(v.shape), -1, axis)


WIDE = False


def mx_kscale(k):
    if not WIDE:
        return np.ones(k)
    levels = np.array([10, -10, 5, -5, 0])
    a = np.random.permutation(np.resize(levels, k // 512 * 4)).reshape(k // 512, 4)
    idx = np.arange(k)
    return np.exp2(a[idx // 512, idx % 128 // 32])


BF16 = ml_dtypes.bfloat16


def bf(x):
    return np.asarray(x, np.float32).astype(BF16)


def f64(x):
    return np.asarray(x).astype(np.float64)


B, S, H, D, M = 2, 512, 16, 128, 1024
E = H * D
R = B * S
EPS = 1e-6


def setup_inputs():
    s = mx_kscale(E)
    return {"query_input": bf(np.random.standard_normal((B, S, E))),
            "norm_query_w": bf((1.0 + 0.1 * np.random.standard_normal(E)) * s),
            "W_in": bf(np.random.standard_normal((E, E)) / np.sqrt(E) / s[None, :])}


def reference(query_input, norm_query_w, W_in):
    x = f64(query_input).reshape(R, E)
    normed = x * (1.0 / np.sqrt(np.mean(x * x, 1, keepdims=True) + EPS))
    h = normed * f64(norm_query_w)
    return (mxq(h, 1, "e4m3") @ mxq(f64(W_in), 1, "e4m3").T).reshape(B, S, E)

@@ -1,0 +1,146 @@
+from contextlib import ExitStack
+
+import concourse.mybir as mybir
+from concourse.masks import make_identity
+
+F32 = mybir.dt.float32
+BF16 = mybir.dt.bfloat16
+U32 = mybir.dt.uint32
+U8 = mybir.dt.uint8
+FP8X4 = mybir.dt.float8_e4m3fn_x4
+ACT = mybir.ActivationFunctionType
+ALU = mybir.AluOpType
+
+P = 128
+R = 1024
+E = 2048
+NB = 512
+EPS = 1e-6
+FLOPS = 2 * R * E * E
+
+SEQ = ("x0", "w0", "x1", "w1", "x2", "w2", "x3", "w3", "x4", "x5", "x6", "x7")
+
+
+def tile_hopfieldmemorylayer_pa_kernel(tc, query_input, norm_query_w, W_in, out):
+    nc = tc.nc
+    x = query_input.flatten_outer_dims()
+    o = out.flatten_outer_dims()
+    with ExitStack() as ctx:
+        const = ctx.enter_context(tc.tile_pool(name="const", bufs=1))
+        xpool = ctx.enter_context(tc.tile_pool(name="xpool", bufs=8))
+        wpool = ctx.enter_context(tc.tile_pool(name="wpool", bufs=16))
+        zpool = ctx.enter_context(tc.tile_pool(name="zpool", bufs=2))
+        small = ctx.enter_context(tc.tile_pool(name="small", bufs=8))
+        ghpool = ctx.enter_context(tc.tile_pool(name="ghpool", bufs=2))
+        gwpool = ctx.enter_context(tc.tile_pool(name="gwpool", bufs=3))
+        respool = ctx.enter_context(tc.tile_pool(name="respool", bufs=6))
+        tps = ctx.enter_context(tc.psum_pool(name="tps", bufs=4))
+        accs = ctx.enter_context(tc.psum_pool(name="accs", bufs=4))
+
+        ident = const.tile([P, P], F32, name="ident")
+        make_identity(nc, ident[:])
+        eps = const.tile([P, 1], F32, name="eps")
+        nc.vector.memset(eps[:], EPS)
+        warm = const.tile([P, 1], F32, name="warm")
+        nc.scalar.activation(out=warm[:], in_=eps[:], func=ACT.Sqrt)
+        graw = const.tile([P, 256], BF16, name="graw")
+        nc.vector.memset(graw[:], 0.0)
+        nc.sync.dma_start(out=graw[0:8, :], in_=norm_query_w.rearrange("(a w) -> a w", w=256))
+        junk = const.tile([P, E], BF16, name="junk")
+        g_t = const.tile([P, 16], F32, name="g_t")
+        hq = const.tile([P, 8, NB], U32, name="hq", align_bytes=64)
+        hs = const.tile([P, 8, NB], U8, name="hs", align_bytes=64)
+        wq = const.tile([P, 4, E], U32, name="wq", align_bytes=64)
+        ws = const.tile([P, 4, E], U8, name="ws", align_bytes=64)
+
+        xt = {}
+        wt = {}
+        for s in SEQ:
+            n = int(s[1:])
+            if s[0] == "x":
+                t = xpool.tile([P, E], BF16, name="xt")
+                nc.sync.dma_start(out=t[:], in_=x[n * P:(n + 1) * P, :])
+                xt[n] = t
+            else:
+                for a in range(4):
+                    t = wpool.tile([P, E], BF16, name="wt")
+                    r0 = n * NB + a * P
+                    nc.sync.dma_start(out=t[:], in_=W_in[r0:r0 + P, :])
+                    wt[(n, a)] = t
+
+        gps = tps.tile([P, P], F32, name="gps", tag="tp")
+        nc.tensor.transpose(gps[:], graw[:].bitcast(F32), ident[:])
+        nc.vector.tensor_copy(out=g_t[:], in_=gps[:, 0:8].bitcast(BF16))
+
+        def prep_x(i):
+            ss = small.tile([P, 1], F32, name="ss")
+            nc.scalar.activation(out=junk[:], in_=xt[i][:], func=ACT.Square, accum_out=ss[:])
+            rms = small.tile([P, 1], F32, name="rms")
+            nc.scalar.activation(out=rms[:], in_=ss[:], func=ACT.Sqrt, bias=eps[:], scale=1.0 / E)
+            rstd = small.tile([P, 1], F32, name="rstd")
+            nc.vector.reciprocal(out=rstd[:], in_=rms[:])
+            z = zpool.tile([P, E], F32, name="z")
+            nc.vector.tensor_scalar(
+                out=z[:].rearrange("p (a e j) -> p a e j", a=8, e=2),
+                in0=xt[i][:].rearrange("p (a j e) -> p a e j", a=8, e=2),
+                scalar1=rstd[:, 0:1], scalar2=None, op0=ALU.mult)
+            gh = ghpool.tile([P, 4, P, 4], BF16, name="gh", align_bytes=64)
+            for c in range(4):
+                bank = tps.tile([P, 4, P], F32, name="xbank", tag="tp")
+                for t in range(4):
+                    col = (4 * c + t) * P
+                    nc.tensor.transpose(bank[:, t, :], z[:, col:col + P], ident[:])
+                nc.vector.tensor_tensor(
+                    out=gh[:, c, :, :], in0=bank[:].rearrange("p t r -> p r t"),
+                    in1=g_t[:, 4 * c:4 * c + 4].unsqueeze(1).to_broadcast([P, P, 4]), op=ALU.mult)
+            nc.vector.quantize_mx(out=hq[:, i, :].bitcast(FP8X4), scales=hs[:, i, :],
+                                  in_=gh[:].rearrange("p c r t -> p (c r t)"))
+
+        def prep_w(j):
+            for c in range(4):
+                gw = gwpool.tile([P, 4 * NB], BF16, name="gw", align_bytes=64)
+                gw32 = gw[:].bitcast(F32).rearrange("p (n u) -> p n u", u=2)
+                for b in range(2):
+                    bank = tps.tile([P, 2, 256], F32, name="wbank", tag="tp")
+                    for u in range(2):
+                        for a in (2 * b, 2 * b + 1):
+                            col = (2 * c + u) * P
+                            nc.tensor.transpose(bank[:, u, (a % 2) * P:(a % 2 + 1) * P],
+                                                wt[(j, a)][:].bitcast(F32)[:, col:col + P], ident[:])
+                    nc.scalar.copy(out=gw32[:, b * 256:(b + 1) * 256, :],
+                                   in_=bank[:].rearrange("p u n -> p n u"))
+                nc.vector.quantize_mx(out=wq[:, c, j * NB:(j + 1) * NB].bitcast(FP8X4),
+                                      scales=ws[:, c, j * NB:(j + 1) * NB], in_=gw[:])
+
+        count = [0]
+
+        def cell(i, j):
+            acc = accs.tile([P, NB], F32, name="acc")
+            for c in range(4):
+                nc.tensor.matmul_mx(
+                    out=acc[:],
+                    lhsT=hq[:, i, c * P:(c + 1) * P].bitcast(FP8X4), lhsT_scale=hs[:, i, c * P:(c + 1) * P],
+                    rhs=wq[:, c, j * NB:(j + 1) * NB].bitcast(FP8X4), rhs_scale=ws[:, c, j * NB:(j + 1) * NB],
+                    start=(c == 0), stop=(c == 3))
+            res = respool.tile([P, NB], F32, name="res")
+            if i >= 4 and count[0] % 2 == 0:
+                nc.vector.tensor_copy(out=res[:], in_=acc[:])
+            else:
+                nc.scalar.copy(out=res[:], in_=acc[:])
+            count[0] += 1
+            nc.sync.dma_start(out=o[i * P:(i + 1) * P, j * NB:(j + 1) * NB], in_=res[:])
+
+        xs = []
+        wsd = []
+        for s in SEQ:
+            n = int(s[1:])
+            if s[0] == "x":
+                prep_x(n)
+                xs.append(n)
+                for j in wsd:
+                    cell(n, j)
+            else:
+                prep_w(n)
+                wsd.append(n)
+                for i in xs:
+                    cell(i, n)

@@ -15,10 +15,11 @@ P = 128
 R = 1024
 E = 2048
 NB = 512
+NH = 256
 EPS = 1e-6
 FLOPS = 2 * R * E * E
 
-SEQ = ("x0", "w0", "x1", "w1", "x2", "w2", "x3", "w3", "x4", "x5", "x6", "x7")
+LOADS = ("x0", "w0", "x1", "w1", "x2", "x3", "w2", "w3", "x4", "x5", "x6", "x7")
 
 
 def tile_hopfieldmemorylayer_pa_kernel(tc, query_input, norm_query_w, W_in, out):
@@ -32,10 +33,11 @@ def tile_hopfieldmemorylayer_pa_kernel(tc, query_input, norm_query_w, W_in, out)
         zpool = ctx.enter_context(tc.tile_pool(name="zpool", bufs=2))
         small = ctx.enter_context(tc.tile_pool(name="small", bufs=8))
         ghpool = ctx.enter_context(tc.tile_pool(name="ghpool", bufs=2))
-        gwpool = ctx.enter_context(tc.tile_pool(name="gwpool", bufs=3))
-        respool = ctx.enter_context(tc.tile_pool(name="respool", bufs=6))
+        gwpool = ctx.enter_context(tc.tile_pool(name="gwpool", bufs=2))
+        respool = ctx.enter_context(tc.tile_pool(name="respool", bufs=8))
         tps = ctx.enter_context(tc.psum_pool(name="tps", bufs=4))
         accs = ctx.enter_context(tc.psum_pool(name="accs", bufs=4))
+        ctx.enter_context(tc.manual_schedule())
 
         ident = const.tile([P, P], F32, name="ident")
         make_identity(nc, ident[:])
@@ -55,7 +57,7 @@ def tile_hopfieldmemorylayer_pa_kernel(tc, query_input, norm_query_w, W_in, out)
 
         xt = {}
         wt = {}
-        for s in SEQ:
+        for s in LOADS:
             n = int(s[1:])
             if s[0] == "x":
                 t = xpool.tile([P, E], BF16, name="xt")
@@ -72,49 +74,78 @@ def tile_hopfieldmemorylayer_pa_kernel(tc, query_input, norm_query_w, W_in, out)
         nc.tensor.transpose(gps[:], graw[:].bitcast(F32), ident[:])
         nc.vector.tensor_copy(out=g_t[:], in_=gps[:, 0:8].bitcast(BF16))
 
-        def prep_x(i):
+        st = {}
+
+        def stats(i):
             ss = small.tile([P, 1], F32, name="ss")
             nc.scalar.activation(out=junk[:], in_=xt[i][:], func=ACT.Square, accum_out=ss[:])
             rms = small.tile([P, 1], F32, name="rms")
             nc.scalar.activation(out=rms[:], in_=ss[:], func=ACT.Sqrt, bias=eps[:], scale=1.0 / E)
+            st[("rms", i)] = rms
+
+        def scale(i):
             rstd = small.tile([P, 1], F32, name="rstd")
-            nc.vector.reciprocal(out=rstd[:], in_=rms[:])
+            nc.vector.reciprocal(out=rstd[:], in_=st[("rms", i)][:])
             z = zpool.tile([P, E], F32, name="z")
             nc.vector.tensor_scalar(
                 out=z[:].rearrange("p (a e j) -> p a e j", a=8, e=2),
                 in0=xt[i][:].rearrange("p (a j e) -> p a e j", a=8, e=2),
                 scalar1=rstd[:, 0:1], scalar2=None, op0=ALU.mult)
-            gh = ghpool.tile([P, 4, P, 4], BF16, name="gh", align_bytes=64)
+            st[("z", i)] = z
+
+        def trx(i):
+            z = st[("z", i)]
+            banks = []
             for c in range(4):
                 bank = tps.tile([P, 4, P], F32, name="xbank", tag="tp")
                 for t in range(4):
                     col = (4 * c + t) * P
                     nc.tensor.transpose(bank[:, t, :], z[:, col:col + P], ident[:])
-                nc.vector.tensor_tensor(
-                    out=gh[:, c, :, :], in0=bank[:].rearrange("p t r -> p r t"),
-                    in1=g_t[:, 4 * c:4 * c + 4].unsqueeze(1).to_broadcast([P, P, 4]), op=ALU.mult)
-            nc.vector.quantize_mx(out=hq[:, i, :].bitcast(FP8X4), scales=hs[:, i, :],
-                                  in_=gh[:].rearrange("p c r t -> p (c r t)"))
+                banks.append(bank)
+            st[("xb", i)] = banks
 
-        def prep_w(j):
+        def outx(i):
+            gh = ghpool.tile([P, 4, P, 4], BF16, name="gh", align_bytes=64)
             for c in range(4):
-                gw = gwpool.tile([P, 4 * NB], BF16, name="gw", align_bytes=64)
-                gw32 = gw[:].bitcast(F32).rearrange("p (n u) -> p n u", u=2)
-                for b in range(2):
-                    bank = tps.tile([P, 2, 256], F32, name="wbank", tag="tp")
-                    for u in range(2):
-                        for a in (2 * b, 2 * b + 1):
-                            col = (2 * c + u) * P
-                            nc.tensor.transpose(bank[:, u, (a % 2) * P:(a % 2 + 1) * P],
-                                                wt[(j, a)][:].bitcast(F32)[:, col:col + P], ident[:])
-                    nc.scalar.copy(out=gw32[:, b * 256:(b + 1) * 256, :],
-                                   in_=bank[:].rearrange("p u n -> p n u"))
-                nc.vector.quantize_mx(out=wq[:, c, j * NB:(j + 1) * NB].bitcast(FP8X4),
-                                      scales=ws[:, c, j * NB:(j + 1) * NB], in_=gw[:])
+                nc.vector.tensor_tensor(
+                    out=gh[:, c, :, :], in0=st[("xb", i)][c][:].rearrange("p t r -> p r t"),
+                    in1=g_t[:, 4 * c:4 * c + 4].unsqueeze(1).to_broadcast([P, P, 4]), op=ALU.mult)
+            st[("gh", i)] = gh
 
-        count = [0]
+        def qx(i):
+            nc.vector.quantize_mx(out=hq[:, i, :].bitcast(FP8X4), scales=hs[:, i, :],
+                                  in_=st[("gh", i)][:].rearrange("p c r t -> p (c r t)"))
 
-        def cell(i, j):
+        def trw(j, h):
+            banks = []
+            for c in range(4):
+                bank = tps.tile([P, 2, NH], F32, name="wbank", tag="tp")
+                for u in range(2):
+                    for a in range(2):
+                        col = (2 * c + u) * P
+                        nc.tensor.transpose(bank[:, u, a * P:(a + 1) * P],
+                                            wt[(j, 2 * h + a)][:].bitcast(F32)[:, col:col + P], ident[:])
+                banks.append(bank)
+            st[("wb", j, h)] = banks
+
+        def outw(j, h, engines):
+            gw = gwpool.tile([P, 4, 4 * NH], BF16, name="gw", align_bytes=64)
+            for c in range(4):
+                dst = gw[:, c, :].bitcast(F32).rearrange("p (n u) -> p n u", u=2)
+                src = st[("wb", j, h)][c][:].rearrange("p u n -> p n u")
+                if engines[c] == "S":
+                    nc.scalar.copy(out=dst, in_=src)
+                else:
+                    nc.vector.tensor_copy(out=dst, in_=src)
+            st[("gw", j, h)] = gw
+
+        def qw(j, h):
+            n0 = j * NB + h * NH
+            for c in range(4):
+                nc.vector.quantize_mx(out=wq[:, c, n0:n0 + NH].bitcast(FP8X4), scales=ws[:, c, n0:n0 + NH],
+                                      in_=st[("gw", j, h)][:, c, :])
+
+        def mm(i, j):
             acc = accs.tile([P, NB], F32, name="acc")
             for c in range(4):
                 nc.tensor.matmul_mx(
@@ -122,25 +153,76 @@ def tile_hopfieldmemorylayer_pa_kernel(tc, query_input, norm_query_w, W_in, out)
                     lhsT=hq[:, i, c * P:(c + 1) * P].bitcast(FP8X4), lhsT_scale=hs[:, i, c * P:(c + 1) * P],
                     rhs=wq[:, c, j * NB:(j + 1) * NB].bitcast(FP8X4), rhs_scale=ws[:, c, j * NB:(j + 1) * NB],
                     start=(c == 0), stop=(c == 3))
+            st[("acc", i, j)] = acc
+
+        def outc(i, j, engine):
             res = respool.tile([P, NB], F32, name="res")
-            if i >= 4 and count[0] % 2 == 0:
-                nc.vector.tensor_copy(out=res[:], in_=acc[:])
+            if engine == "S":
+                nc.scalar.copy(out=res[:], in_=st[("acc", i, j)][:])
             else:
-                nc.scalar.copy(out=res[:], in_=acc[:])
-            count[0] += 1
+                nc.vector.tensor_copy(out=res[:], in_=st[("acc", i, j)][:])
             nc.sync.dma_start(out=o[i * P:(i + 1) * P, j * NB:(j + 1) * NB], in_=res[:])
 
-        xs = []
-        wsd = []
-        for s in SEQ:
-            n = int(s[1:])
-            if s[0] == "x":
-                prep_x(n)
-                xs.append(n)
-                for j in wsd:
-                    cell(n, j)
-            else:
-                prep_w(n)
-                wsd.append(n)
-                for i in xs:
-                    cell(i, n)
+        stats(0)
+        trw(0, 0)
+        scale(0)
+        outw(0, 0, "SSSS")
+        trx(0)
+        stats(1)
+        qw(0, 0)
+        outx(0)
+        trw(0, 1)
+        scale(1)
+        qx(0)
+        outw(0, 1, "SSSS")
+        trx(1)
+        stats(2)
+        outx(1)
+        trw(1, 0)
+        qw(0, 1)
+        qx(1)
+        mm(0, 0)
+        outw(1, 0, "SSSS")
+        scale(2)
+        outc(0, 0, "S")
+        units = ((1, 1), (2, 0), (2, 1), (3, 0), (3, 1))
+        cells = ((1, 0), (0, 1), (1, 1), (0, 2), (1, 2))
+        prev = (1, 0)
+        for n in range(5):
+            trw(units[n][0], units[n][1])
+            qw(prev[0], prev[1])
+            mm(cells[n][0], cells[n][1])
+            outw(units[n][0], units[n][1], "VSVS")
+            if n == 0:
+                stats(3)
+            if n == 4:
+                stats(4)
+                stats(5)
+            outc(cells[n][0], cells[n][1], "S")
+            prev = units[n]
+        trx(2)
+        qw(3, 1)
+        scale(3)
+        outx(2)
+        mm(0, 3)
+        mm(1, 3)
+        qx(2)
+        outc(0, 3, "S")
+        outc(1, 3, "S")
+        stats(6)
+        for i in range(3, 8):
+            trx(i)
+            if i < 7:
+                scale(i + 1)
+            outx(i)
+            for j in range(4):
+                mm(i - 1, j)
+            qx(i)
+            for j in range(4):
+                outc(i - 1, j, "S")
+            if i == 3:
+                stats(7)
+        for j in range(4):
+            mm(7, j)
+        for j in range(4):
+            outc(7, j, "V" if j % 2 else "S")

@@ -177,29 +177,35 @@ def tile_hopfieldmemorylayer_pa_kernel(tc, query_input, norm_query_w, W_in, out)
         outw(0, 1, "SSSS")
         trx(1)
         stats(2)
+        qw(0, 1)
+        mm(0, 0)
         outx(1)
         trw(1, 0)
-        qw(0, 1)
         qx(1)
-        mm(0, 0)
+        outc(0, 0, "S")
         outw(1, 0, "SSSS")
         scale(2)
-        outc(0, 0, "S")
-        units = ((1, 1), (2, 0), (2, 1), (3, 0), (3, 1))
-        cells = ((1, 0), (0, 1), (1, 1), (0, 2), (1, 2))
-        prev = (1, 0)
-        for n in range(5):
-            trw(units[n][0], units[n][1])
-            qw(prev[0], prev[1])
-            mm(cells[n][0], cells[n][1])
-            outw(units[n][0], units[n][1], "VSVS")
-            if n == 0:
+        trw(1, 1)
+        qw(1, 0)
+        mm(1, 0)
+        outw(1, 1, "VSVS")
+        outc(1, 0, "S")
+        for j in range(2, 4):
+            trw(j, 0)
+            qw(j - 1, 1)
+            outw(j, 0, "SVSV")
+            trw(j, 1)
+            mm(0, j - 1)
+            mm(1, j - 1)
+            outw(j, 1, "SVSV")
+            qw(j, 0)
+            if j == 3:
                 stats(3)
-            if n == 4:
+            outc(0, j - 1, "S")
+            outc(1, j - 1, "S")
+            if j == 3:
                 stats(4)
                 stats(5)
-            outc(cells[n][0], cells[n][1], "S")
-            prev = units[n]
         trx(2)
         qw(3, 1)
         scale(3)
@@ -212,11 +218,11 @@ def tile_hopfieldmemorylayer_pa_kernel(tc, query_input, norm_query_w, W_in, out)
         stats(6)
         for i in range(3, 8):
             trx(i)
-            if i < 7:
-                scale(i + 1)
             outx(i)
             for j in range(4):
                 mm(i - 1, j)
+            if i < 7:
+                scale(i + 1)
             qx(i)
             for j in range(4):
                 outc(i - 1, j, "S")

@@ -57,18 +57,30 @@ def tile_hopfieldmemorylayer_pa_kernel(tc, query_input, norm_query_w, W_in, out)
 
         xt = {}
         wt = {}
+        EH = E // 2
         for s in LOADS:
             n = int(s[1:])
             if s[0] == "x":
                 t = xpool.tile([P, E], BF16, name="xt")
-                nc.sync.dma_start(out=t[:], in_=x[n * P:(n + 1) * P, :])
+                if n == 0:
+                    nc.sync.dma_start(out=t[:, 0:EH], in_=x[0:P, 0:EH])
+                    nc.sync.dma_start(out=t[:, EH:E], in_=x[0:P, EH:E])
+                else:
+                    nc.sync.dma_start(out=t[:], in_=x[n * P:(n + 1) * P, :])
                 xt[n] = t
             else:
                 for a in range(4):
                     t = wpool.tile([P, E], BF16, name="wt")
-                    r0 = n * NB + a * P
-                    nc.sync.dma_start(out=t[:], in_=W_in[r0:r0 + P, :])
                     wt[(n, a)] = t
+                if n == 0:
+                    for half in range(2):
+                        for a in range(2):
+                            nc.sync.dma_start(out=wt[(0, a)][:, half * EH:(half + 1) * EH],
+                                              in_=W_in[a * P:(a + 1) * P, half * EH:(half + 1) * EH])
+                for a in range(4):
+                    if n > 0 or a >= 2:
+                        r0 = n * NB + a * P
+                        nc.sync.dma_start(out=wt[(n, a)][:], in_=W_in[r0:r0 + P, :])
 
         gps = tps.tile([P, P], F32, name="gps", tag="tp")
         nc.tensor.transpose(gps[:], graw[:].bitcast(F32), ident[:])
@@ -78,9 +90,17 @@ def tile_hopfieldmemorylayer_pa_kernel(tc, query_input, norm_query_w, W_in, out)
 
         def stats(i):
             ss = small.tile([P, 1], F32, name="ss")
-            nc.scalar.activation(out=junk[:], in_=xt[i][:], func=ACT.Square, accum_out=ss[:])
             rms = small.tile([P, 1], F32, name="rms")
-            nc.scalar.activation(out=rms[:], in_=ss[:], func=ACT.Sqrt, bias=eps[:], scale=1.0 / E)
+            if i == 0:
+                nc.scalar.activation(out=junk[:, 0:EH], in_=xt[i][:, 0:EH], func=ACT.Square, accum_out=ss[:])
+                ss2 = const.tile([P, 1], F32, name="ss2")
+                nc.scalar.activation(out=junk[:, EH:E], in_=xt[i][:, EH:E], func=ACT.Square, accum_out=ss2[:])
+                part = const.tile([P, 1], F32, name="part")
+                nc.scalar.activation(out=part[:], in_=ss2[:], func=ACT.Identity, bias=eps[:], scale=1.0 / E)
+                nc.scalar.activation(out=rms[:], in_=ss[:], func=ACT.Sqrt, bias=part[:], scale=1.0 / E)
+            else:
+                nc.scalar.activation(out=junk[:], in_=xt[i][:], func=ACT.Square, accum_out=ss[:])
+                nc.scalar.activation(out=rms[:], in_=ss[:], func=ACT.Sqrt, bias=eps[:], scale=1.0 / E)
             st[("rms", i)] = rms
 
         def scale(i):
@@ -177,35 +197,29 @@ def tile_hopfieldmemorylayer_pa_kernel(tc, query_input, norm_query_w, W_in, out)
         outw(0, 1, "SSSS")
         trx(1)
         stats(2)
-        qw(0, 1)
-        mm(0, 0)
         outx(1)
         trw(1, 0)
+        qw(0, 1)
         qx(1)
-        outc(0, 0, "S")
+        mm(0, 0)
         outw(1, 0, "SSSS")
         scale(2)
-        trw(1, 1)
-        qw(1, 0)
-        mm(1, 0)
-        outw(1, 1, "VSVS")
-        outc(1, 0, "S")
-        for j in range(2, 4):
-            trw(j, 0)
-            qw(j - 1, 1)
-            outw(j, 0, "SVSV")
-            trw(j, 1)
-            mm(0, j - 1)
-            mm(1, j - 1)
-            outw(j, 1, "SVSV")
-            qw(j, 0)
-            if j == 3:
+        outc(0, 0, "S")
+        units = ((1, 1), (2, 0), (2, 1), (3, 0), (3, 1))
+        cells = ((1, 0), (0, 1), (1, 1), (0, 2), (1, 2))
+        prev = (1, 0)
+        for n in range(5):
+            trw(units[n][0], units[n][1])
+            qw(prev[0], prev[1])
+            mm(cells[n][0], cells[n][1])
+            outw(units[n][0], units[n][1], "VSVS")
+            if n == 0:
                 stats(3)
-            outc(0, j - 1, "S")
-            outc(1, j - 1, "S")
-            if j == 3:
+            if n == 4:
                 stats(4)
                 stats(5)
+            outc(cells[n][0], cells[n][1], "S")
+            prev = units[n]
         trx(2)
         qw(3, 1)
         scale(3)
@@ -218,17 +232,36 @@ def tile_hopfieldmemorylayer_pa_kernel(tc, query_input, norm_query_w, W_in, out)
         stats(6)
         for i in range(3, 8):
             trx(i)
+            if i < 7:
+                scale(i + 1)
             outx(i)
             for j in range(4):
                 mm(i - 1, j)
-            if i < 7:
-                scale(i + 1)
             qx(i)
             for j in range(4):
                 outc(i - 1, j, "S")
             if i == 3:
                 stats(7)
-        for j in range(4):
+        for j in range(3):
             mm(7, j)
-        for j in range(4):
+        halves = []
+        for h in range(2):
+            acc = accs.tile([P, NH], F32, name="acch", tag="acc")
+            n0 = 3 * NB + h * NH
+            for c in range(4):
+                nc.tensor.matmul_mx(
+                    out=acc[:],
+                    lhsT=hq[:, 7, c * P:(c + 1) * P].bitcast(FP8X4), lhsT_scale=hs[:, 7, c * P:(c + 1) * P],
+                    rhs=wq[:, c, n0:n0 + NH].bitcast(FP8X4), rhs_scale=ws[:, c, n0:n0 + NH],
+                    start=(c == 0), stop=(c == 3))
+            halves.append(acc)
+        for j in range(3):
             outc(7, j, "V" if j % 2 else "S")
+        for h in range(2):
+            res = respool.tile([P, NH], F32, name="resh", tag="res")
+            if h == 0:
+                nc.vector.tensor_copy(out=res[:], in_=halves[h][:])
+            else:
+                nc.scalar.copy(out=res[:], in_=halves[h][:])
+            n0 = 3 * NB + h * NH
+            nc.sync.dma_start(out=o[7 * P:8 * P, n0:n0 + NH], in_=res[:])

@@ -197,14 +197,14 @@ def tile_hopfieldmemorylayer_pa_kernel(tc, query_input, norm_query_w, W_in, out)
         outw(0, 1, "SSSS")
         trx(1)
         stats(2)
+        qw(0, 1)
+        mm(0, 0)
         outx(1)
         trw(1, 0)
-        qw(0, 1)
         qx(1)
-        mm(0, 0)
+        outc(0, 0, "S")
         outw(1, 0, "SSSS")
         scale(2)
-        outc(0, 0, "S")
         units = ((1, 1), (2, 0), (2, 1), (3, 0), (3, 1))
         cells = ((1, 0), (0, 1), (1, 1), (0, 2), (1, 2))
         prev = (1, 0)

from contextlib import ExitStack

import concourse.mybir as mybir
from concourse.masks import make_identity

F32 = mybir.dt.float32
BF16 = mybir.dt.bfloat16
U32 = mybir.dt.uint32
U8 = mybir.dt.uint8
FP8X4 = mybir.dt.float8_e4m3fn_x4
ACT = mybir.ActivationFunctionType
ALU = mybir.AluOpType

P = 128
R = 1024
E = 2048
NB = 512
NH = 256
EPS = 1e-6
FLOPS = 2 * R * E * E

LOADS = ("x0", "w0", "x1", "w1", "x2", "x3", "w2", "w3", "x4", "x5", "x6", "x7")


def tile_hopfieldmemorylayer_pa_kernel(tc, query_input, norm_query_w, W_in, out):
    nc = tc.nc
    x = query_input.flatten_outer_dims()
    o = out.flatten_outer_dims()
    with ExitStack() as ctx:
        const = ctx.enter_context(tc.tile_pool(name="const", bufs=1))
        xpool = ctx.enter_context(tc.tile_pool(name="xpool", bufs=8))
        wpool = ctx.enter_context(tc.tile_pool(name="wpool", bufs=16))
        zpool = ctx.enter_context(tc.tile_pool(name="zpool", bufs=2))
        small = ctx.enter_context(tc.tile_pool(name="small", bufs=8))
        ghpool = ctx.enter_context(tc.tile_pool(name="ghpool", bufs=2))
        gwpool = ctx.enter_context(tc.tile_pool(name="gwpool", bufs=2))
        respool = ctx.enter_context(tc.tile_pool(name="respool", bufs=8))
        tps = ctx.enter_context(tc.psum_pool(name="tps", bufs=4))
        accs = ctx.enter_context(tc.psum_pool(name="accs", bufs=4))
        ctx.enter_context(tc.manual_schedule())

        ident = const.tile([P, P], F32, name="ident")
        make_identity(nc, ident[:])
        eps = const.tile([P, 1], F32, name="eps")
        nc.vector.memset(eps[:], EPS)
        warm = const.tile([P, 1], F32, name="warm")
        nc.scalar.activation(out=warm[:], in_=eps[:], func=ACT.Sqrt)
        graw = const.tile([P, 256], BF16, name="graw")
        nc.vector.memset(graw[:], 0.0)
        nc.sync.dma_start(out=graw[0:8, :], in_=norm_query_w.rearrange("(a w) -> a w", w=256))
        junk = const.tile([P, E], BF16, name="junk")
        g_t = const.tile([P, 16], F32, name="g_t")
        hq = const.tile([P, 8, NB], U32, name="hq", align_bytes=64)
        hs = const.tile([P, 8, NB], U8, name="hs", align_bytes=64)
        wq = const.tile([P, 4, E], U32, name="wq", align_bytes=64)
        ws = const.tile([P, 4, E], U8, name="ws", align_bytes=64)

        xt = {}
        wt = {}
        EH = E // 2
        for s in LOADS:
            n = int(s[1:])
            if s[0] == "x":
                t = xpool.tile([P, E], BF16, name="xt")
                if n == 0:
                    nc.sync.dma_start(out=t[:, 0:EH], in_=x[0:P, 0:EH])
                    nc.sync.dma_start(out=t[:, EH:E], in_=x[0:P, EH:E])
                else:
                    nc.sync.dma_start(out=t[:], in_=x[n * P:(n + 1) * P, :])
                xt[n] = t
            else:
                for a in range(4):
                    t = wpool.tile([P, E], BF16, name="wt")
                    wt[(n, a)] = t
                if n == 0:
                    for half in range(2):
                        for a in range(2):
                            nc.sync.dma_start(out=wt[(0, a)][:, half * EH:(half + 1) * EH],
                                              in_=W_in[a * P:(a + 1) * P, half * EH:(half + 1) * EH])
                for a in range(4):
                    if n > 0 or a >= 2:
                        r0 = n * NB + a * P
                        nc.sync.dma_start(out=wt[(n, a)][:], in_=W_in[r0:r0 + P, :])

        gps = tps.tile([P, P], F32, name="gps", tag="tp")
        nc.tensor.transpose(gps[:], graw[:].bitcast(F32), ident[:])
        nc.vector.tensor_copy(out=g_t[:], in_=gps[:, 0:8].bitcast(BF16))

        st = {}

        def stats(i):
            ss = small.tile([P, 1], F32, name="ss")
            rms = small.tile([P, 1], F32, name="rms")
            if i == 0:
                nc.scalar.activation(out=junk[:, 0:EH], in_=xt[i][:, 0:EH], func=ACT.Square, accum_out=ss[:])
                ss2 = const.tile([P, 1], F32, name="ss2")
                nc.scalar.activation(out=junk[:, EH:E], in_=xt[i][:, EH:E], func=ACT.Square, accum_out=ss2[:])
                part = const.tile([P, 1], F32, name="part")
                nc.scalar.activation(out=part[:], in_=ss2[:], func=ACT.Identity, bias=eps[:], scale=1.0 / E)
                nc.scalar.activation(out=rms[:], in_=ss[:], func=ACT.Sqrt, bias=part[:], scale=1.0 / E)
            else:
                nc.scalar.activation(out=junk[:], in_=xt[i][:], func=ACT.Square, accum_out=ss[:])
                nc.scalar.activation(out=rms[:], in_=ss[:], func=ACT.Sqrt, bias=eps[:], scale=1.0 / E)
            st[("rms", i)] = rms

        def scale(i):
            rstd = small.tile([P, 1], F32, name="rstd")
            nc.vector.reciprocal(out=rstd[:], in_=st[("rms", i)][:])
            z = zpool.tile([P, E], F32, name="z")
            nc.vector.tensor_scalar(
                out=z[:].rearrange("p (a e j) -> p a e j", a=8, e=2),
                in0=xt[i][:].rearrange("p (a j e) -> p a e j", a=8, e=2),
                scalar1=rstd[:, 0:1], scalar2=None, op0=ALU.mult)
            st[("z", i)] = z

        def trx(i):
            z = st[("z", i)]
            banks = []
            for c in range(4):
                bank = tps.tile([P, 4, P], F32, name="xbank", tag="tp")
                for t in range(4):
                    col = (4 * c + t) * P
                    nc.tensor.transpose(bank[:, t, :], z[:, col:col + P], ident[:])
                banks.append(bank)
            st[("xb", i)] = banks

        def outx(i):
            gh = ghpool.tile([P, 4, P, 4], BF16, name="gh", align_bytes=64)
            for c in range(4):
                nc.vector.tensor_tensor(
                    out=gh[:, c, :, :], in0=st[("xb", i)][c][:].rearrange("p t r -> p r t"),
                    in1=g_t[:, 4 * c:4 * c + 4].unsqueeze(1).to_broadcast([P, P, 4]), op=ALU.mult)
            st[("gh", i)] = gh

        def qx(i):
            nc.vector.quantize_mx(out=hq[:, i, :].bitcast(FP8X4), scales=hs[:, i, :],
                                  in_=st[("gh", i)][:].rearrange("p c r t -> p (c r t)"))

        def trw(j, h):
            banks = []
            for c in range(4):
                bank = tps.tile([P, 2, NH], F32, name="wbank", tag="tp")
                for u in range(2):
                    for a in range(2):
                        col = (2 * c + u) * P
                        nc.tensor.transpose(bank[:, u, a * P:(a + 1) * P],
                                            wt[(j, 2 * h + a)][:].bitcast(F32)[:, col:col + P], ident[:])
                banks.append(bank)
            st[("wb", j, h)] = banks

        def outw(j, h, engines):
            gw = gwpool.tile([P, 4, 4 * NH], BF16, name="gw", align_bytes=64)
            for c in range(4):
                dst = gw[:, c, :].bitcast(F32).rearrange("p (n u) -> p n u", u=2)
                src = st[("wb", j, h)][c][:].rearrange("p u n -> p n u")
                if engines[c] == "S":
                    nc.scalar.copy(out=dst, in_=src)
                else:
                    nc.vector.tensor_copy(out=dst, in_=src)
            st[("gw", j, h)] = gw

        def qw(j, h):
            n0 = j * NB + h * NH
            for c in range(4):
                nc.vector.quantize_mx(out=wq[:, c, n0:n0 + NH].bitcast(FP8X4), scales=ws[:, c, n0:n0 + NH],
                                      in_=st[("gw", j, h)][:, c, :])

        def mm(i, j):
            acc = accs.tile([P, NB], F32, name="acc")
            for c in range(4):
                nc.tensor.matmul_mx(
                    out=acc[:],
                    lhsT=hq[:, i, c * P:(c + 1) * P].bitcast(FP8X4), lhsT_scale=hs[:, i, c * P:(c + 1) * P],
                    rhs=wq[:, c, j * NB:(j + 1) * NB].bitcast(FP8X4), rhs_scale=ws[:, c, j * NB:(j + 1) * NB],
                    start=(c == 0), stop=(c == 3))
            st[("acc", i, j)] = acc

        def outc(i, j, engine):
            res = respool.tile([P, NB], F32, name="res")
            if engine == "S":
                nc.scalar.copy(out=res[:], in_=st[("acc", i, j)][:])
            else:
                nc.vector.tensor_copy(out=res[:], in_=st[("acc", i, j)][:])
            nc.sync.dma_start(out=o[i * P:(i + 1) * P, j * NB:(j + 1) * NB], in_=res[:])

        stats(0)
        trw(0, 0)
        scale(0)
        outw(0, 0, "SSSS")
        trx(0)
        stats(1)
        qw(0, 0)
        outx(0)
        trw(0, 1)
        scale(1)
        qx(0)
        outw(0, 1, "SSSS")
        trx(1)
        stats(2)
        qw(0, 1)
        mm(0, 0)
        outx(1)
        trw(1, 0)
        qx(1)
        outc(0, 0, "S")
        outw(1, 0, "SSSS")
        scale(2)
        units = ((1, 1), (2, 0), (2, 1), (3, 0), (3, 1))
        cells = ((1, 0), (0, 1), (1, 1), (0, 2), (1, 2))
        prev = (1, 0)
        for n in range(5):
            trw(units[n][0], units[n][1])
            qw(prev[0], prev[1])
            mm(cells[n][0], cells[n][1])
            outw(units[n][0], units[n][1], "VSVS")
            if n == 0:
                stats(3)
            if n == 4:
                stats(4)
                stats(5)
            outc(cells[n][0], cells[n][1], "S")
            prev = units[n]
        trx(2)
        qw(3, 1)
        scale(3)
        outx(2)
        mm(0, 3)
        mm(1, 3)
        qx(2)
        outc(0, 3, "S")
        outc(1, 3, "S")
        stats(6)
        for i in range(3, 8):
            trx(i)
            if i < 7:
                scale(i + 1)
            outx(i)
            for j in range(4):
                mm(i - 1, j)
            qx(i)
            for j in range(4):
                outc(i - 1, j, "S")
            if i == 3:
                stats(7)
        for j in range(3):
            mm(7, j)
        halves = []
        for h in range(2):
            acc = accs.tile([P, NH], F32, name="acch", tag="acc")
            n0 = 3 * NB + h * NH
            for c in range(4):
                nc.tensor.matmul_mx(
                    out=acc[:],
                    lhsT=hq[:, 7, c * P:(c + 1) * P].bitcast(FP8X4), lhsT_scale=hs[:, 7, c * P:(c + 1) * P],
                    rhs=wq[:, c, n0:n0 + NH].bitcast(FP8X4), rhs_scale=ws[:, c, n0:n0 + NH],
                    start=(c == 0), stop=(c == 3))
            halves.append(acc)
        for j in range(3):
            outc(7, j, "V" if j % 2 else "S")
        for h in range(2):
            res = respool.tile([P, NH], F32, name="resh", tag="res")
            if h == 0:
                nc.vector.tensor_copy(out=res[:], in_=halves[h][:])
            else:
                nc.scalar.copy(out=res[:], in_=halves[h][:])
            n0 = 3 * NB + h * NH
            nc.sync.dma_start(out=o[7 * P:8 * P, n0:n0 + NH], in_=res[:])
